import numpy as np
import ml_dtypes


BF16 = ml_dtypes.bfloat16


def bf(x):
    return np.asarray(x, np.float32).astype(BF16)


def f64(x):
    return np.asarray(x).astype(np.float64)


E2M1 = np.array([0.0, 0.5, 1.0, 1.5, 2.0, 3.0, 4.0, 6.0, -0.0, -0.5, -1.0, -1.5, -2.0, -3.0, -4.0, -6.0])


def pack_weight(w, fmt):
    k, n = w.shape
    w = f64(bf(w)).reshape(k // 32, 32, n)
    amax = np.abs(w).max(1)
    if fmt == "e4m3":
        byte = np.frexp(amax)[1] - 1 + 127 - 7
    else:
        mant, ex = np.frexp(amax / 6.0)
        byte = np.where(mant > 0.5, ex, ex - 1) + 127
    byte = np.clip(np.where(amax > 0, byte, 1), 1, 254)
    scaled = (w * np.exp2(127.0 - byte)[:, None, :]).reshape(k, n).astype(np.float32)
    by_word = np.ascontiguousarray(scaled.reshape(k // 512, 128, 4, n).transpose(0, 1, 3, 2))
    if fmt == "e4m3":
        words = by_word.astype(ml_dtypes.float8_e4m3fn).view(np.uint8)
    else:
        c = by_word.astype(ml_dtypes.float4_e2m1fn).view(np.uint8) & 0xF
        words = c[..., 0::2] | (c[..., 1::2] << 4)
    return np.ascontiguousarray(words), np.ascontiguousarray(byte.astype(np.uint8).reshape(k // 512, 16, n))


def unpack_weight(words, scales, fmt):
    g, p, n, _ = words.shape
    if fmt == "e4m3":
        vals = np.ascontiguousarray(words).view(ml_dtypes.float8_e4m3fn).astype(np.float64)
    else:
        nib = np.empty((g, p, n, 4), np.uint8)
        nib[..., 0::2] = words & 0xF
        nib[..., 1::2] = words >> 4
        vals = E2M1[nib]
    vals = vals * np.repeat(np.exp2(scales.astype(np.float64) - 127.0), 8, axis=1)[..., None]
    return vals.transpose(0, 1, 3, 2).reshape(g * 512, n)

def pack4(w):
    words, scales = pack_weight(w, "e2m1")
    return words.reshape(words.shape[0], 128, -1), scales


def unpack4(words, scales):
    return unpack_weight(words.reshape(words.shape[0], 128, -1, 2), scales, "e2m1")


def kspread(k):
    return np.exp2(np.repeat(np.random.randint(-6, 7, k // 32), 32).astype(np.float64))


B, IN, OUT = 512, 3072, 1536


def setup_inputs():
    s = kspread(IN)
    input_data = np.random.standard_normal((B, IN)) * s
    input_data_words, input_data_scales = pack4(input_data.T)
    weight_words, weight_scales = pack4((np.random.standard_normal((OUT, IN)) / np.sqrt(IN) / s).T)
    bias = bf(np.random.standard_normal(OUT) * 0.5)
    prev_grad = np.random.standard_normal((OUT, IN)) / np.sqrt(IN) / s
    prev_grad_words, prev_grad_scales = pack4(prev_grad.T)
    return {"input_data_words": input_data_words,
            "input_data_scales": input_data_scales,
            "weight_words": weight_words,
            "weight_scales": weight_scales,
            "bias": bias,
            "prev_grad_words": prev_grad_words,
            "prev_grad_scales": prev_grad_scales,
            "prev_bias_grad": bf(np.random.standard_normal(OUT) * 0.5),
            "lr_samples": bf(np.random.uniform(0.1, 1.0, B))}


def reference(input_data_words, input_data_scales, weight_words, weight_scales, bias, prev_grad_words, prev_grad_scales, prev_bias_grad, lr_samples):
    xq = unpack4(input_data_words, input_data_scales).T
    base = (xq @ unpack4(weight_words, weight_scales)) + f64(bias)
    pert = (xq @ unpack4(prev_grad_words, prev_grad_scales)) + f64(prev_bias_grad)
    return base - f64(lr_samples)[:, None] * pert

@@ -1,0 +1,183 @@
+from contextlib import ExitStack
+
+import concourse.mybir as mybir
+
+F32 = mybir.dt.float32
+BF16 = mybir.dt.bfloat16
+U8 = mybir.dt.uint8
+I32 = mybir.dt.int32
+FP4X4 = mybir.dt.float4_e2m1fn_x4
+ALU = mybir.AluOpType
+ACT = mybir.ActivationFunctionType
+
+B, IN, OUT = 512, 3072, 1536
+FLOPS = 2 * 2 * B * IN * OUT
+
+P = 128
+G = IN // 512
+T = B // P
+NB = 512
+N_BLOCKS = OUT // NB
+WARM = 11
+
+
+def tile_optimizedlinear_kernel(
+    tc, x_words, x_scales, w_words, w_scales, bias, y_words, y_scales, prev_bias, lr, out
+):
+    nc = tc.nc
+    with ExitStack() as ctx:
+        keep = ctx.enter_context(tc.tile_pool(name="keep", bufs=1))
+        outs = ctx.enter_context(tc.tile_pool(name="outs", bufs=6))
+        psum = ctx.enter_context(tc.psum_pool(name="psum", bufs=8))
+        ctx.enter_context(tc.manual_schedule())
+
+        def keep_tile(name, shape, dtype):
+            return keep.tile(shape, dtype, name=name, align_bytes=256)
+
+        def load_codes(dst, src):
+            nc.sync.dma_start(out=dst.bitcast(I32), in_=src.bitcast(I32))
+
+        def load_scales(plane, scales, g0, g1, c0, c1):
+            for q in range(4):
+                src = scales[g0:g1, 4 * q : 4 * q + 4, c0:c1].rearrange("g r n -> r g n")
+                nc.sync.dma_start(out=plane[32 * q : 32 * q + 4, :, :].bitcast(I32), in_=src.bitcast(I32))
+
+        def zero(plane):
+            nc.vector.memset(plane[:].rearrange("p g n -> p (g n)").bitcast(I32), 0)
+
+        warm = keep_tile("warm", [P, NB], BF16)
+        lr_bf = keep_tile("lr_bf", [P, T], BF16)
+        lr_col = keep_tile("lr_col", [P, T], F32)
+        spread = [keep_tile("prev_bias_b", [P, OUT], BF16), keep_tile("bias_b", [P, OUT], BF16)]
+        xc = [keep_tile("xc%d" % g, [P, 2 * B], U8) for g in range(3)]
+        xc35 = keep_tile("xc35", [P, 3, 2 * B], U8)
+        ya0 = [keep_tile("ya0_%d" % n, [P, 2 * NB], U8) for n in range(2)]
+        ya = [None] + [keep_tile("ya%d" % g, [P, 4 * NB], U8) for g in range(1, G)]
+        yb = keep_tile("yb", [P, G, 2 * NB], U8)
+        wc = [keep_tile("wc%d" % g, [P, 2 * OUT], U8) for g in range(G)]
+        xs = keep_tile("xs", [P, G, B], U8)
+        ysa01 = keep_tile("ysa01", [P, 2, 2 * NB], U8)
+        ysa25 = keep_tile("ysa25", [P, 4, 2 * NB], U8)
+        ysb = keep_tile("ysb", [P, G, NB], U8)
+        ws = keep_tile("ws", [P, G, OUT], U8)
+
+        nc.gpsimd.memset(warm[:], 0.0)
+        zero(ysa01)
+        zero(xs)
+        nc.gpsimd.dma_start(out=lr_bf[:], in_=lr.rearrange("(t p) -> p t", p=P))
+
+        load_codes(xc[0][:], x_words[0])
+        load_codes(ya0[0][:], y_words[0][:, 0 : 2 * NB])
+        load_scales(ysa01, y_scales, 0, 2, 0, 2 * NB)
+        load_scales(xs, x_scales, 0, G, 0, B)
+        load_codes(ya0[1][:], y_words[0][:, 2 * NB : 4 * NB])
+        load_codes(xc[1][:], x_words[1])
+        load_codes(ya[1][:], y_words[1][:, 0 : 4 * NB])
+        zero(ysa25)
+        load_scales(ysa25, y_scales, 2, G, 0, 2 * NB)
+        load_codes(xc[2][:], x_words[2])
+        load_codes(ya[2][:], y_words[2][:, 0 : 4 * NB])
+        load_codes(xc35[:], x_words[3:6].rearrange("g p c -> p g c"))
+        for g in (3, 4, 5):
+            load_codes(ya[g][:], y_words[g][:, 0 : 4 * NB])
+        nc.sync.dma_start(out=spread[0][:], in_=prev_bias.partition_broadcast(P))
+        nc.sync.dma_start(out=spread[1][:], in_=bias.partition_broadcast(P))
+        zero(ysb)
+        load_scales(ysb, y_scales, 0, G, 2 * NB, 3 * NB)
+        load_codes(yb[:], y_words.rearrange("g p c -> p g c")[:, :, 4 * NB : 6 * NB])
+        zero(ws)
+        load_scales(ws, w_scales, 0, G, 0, OUT)
+        for g in range(G):
+            load_codes(wc[g][:], w_words[g])
+
+        def x_op(g, t):
+            codes = xc[g][:, 256 * t : 256 * (t + 1)] if g < 3 else xc35[:, g - 3, 256 * t : 256 * (t + 1)]
+            return codes.bitcast(FP4X4), xs[:, g, P * t : P * (t + 1)]
+
+        def y_op(g, n):
+            if n == 2:
+                return yb[:, g, :].bitcast(FP4X4), ysb[:, g, :]
+            codes = ya0[n][:] if g == 0 else ya[g][:, 2 * NB * n : 2 * NB * (n + 1)]
+            plane = ysa01[:, g, NB * n : NB * (n + 1)] if g < 2 else ysa25[:, g - 2, NB * n : NB * (n + 1)]
+            return codes.bitcast(FP4X4), plane
+
+        def w_op(g, c0, width):
+            return wc[g][:, 2 * c0 : 2 * (c0 + width)].bitcast(FP4X4), ws[:, g, c0 : c0 + width]
+
+        def one_pass(acc, stationary, moving, g):
+            nc.tensor.matmul_mx(
+                out=acc,
+                lhsT=stationary[0],
+                lhsT_scale=stationary[1],
+                rhs=moving[0],
+                rhs_scale=moving[1],
+                start=(g == 0),
+                stop=(g == G - 1),
+            )
+
+        nc.vector.tensor_copy(out=lr_col[:], in_=lr_bf[:])
+        acc = psum.tile([P, NB], F32, name="acc")
+        for i in range(WARM):
+            nc.tensor.matmul(out=acc[:], lhsT=warm[:, 0:P], rhs=warm[:], start=True, stop=True)
+
+        shift = {}
+        for n in range(N_BLOCKS):
+            cols = slice(NB * n, NB * (n + 1))
+            for t in range(T):
+                s = keep_tile("shift%d_%d" % (n, t), [P, NB], F32)
+                nc.vector.scalar_tensor_tensor(
+                    out=s[:],
+                    in0=spread[0][:, cols],
+                    scalar=lr_col[:, t : t + 1],
+                    in1=spread[1][:, cols],
+                    op0=ALU.mult,
+                    op1=ALU.subtract,
+                )
+                shift[n, t] = s
+
+        update = {}
+
+        def finish_pert(acc, n, t):
+            u = keep_tile("update%d_%d" % (n, t), [P, NB], F32)
+            nc.vector.scalar_tensor_tensor(
+                out=u[:],
+                in0=acc[:],
+                scalar=lr_col[:, t : t + 1],
+                in1=shift[n, t][:],
+                op0=ALU.mult,
+                op1=ALU.add,
+            )
+            update[n, t] = u
+
+        first = [(n, t) for n in range(2) for t in range(T)]
+        accs = {}
+        for g in range(4):
+            for n, t in first:
+                if g == 0:
+                    acc = psum.tile([P, NB], F32, name="acc")
+                    accs[n, t] = acc
+                one_pass(accs[n, t][:], x_op(g, t), y_op(g, n), g)
+        for n, t in first:
+            for g in range(4, G):
+                one_pass(accs[n, t][:], x_op(g, t), y_op(g, n), g)
+            finish_pert(accs[n, t], n, t)
+        for t in range(T):
+            acc = psum.tile([P, NB], F32, name="acc")
+            for g in range(G):
+                one_pass(acc[:], x_op(g, t), y_op(g, 2), g)
+            finish_pert(acc, 2, t)
+
+        for n in range(N_BLOCKS):
+            for t in range(T):
+                last = n == N_BLOCKS - 1 and t == T - 1
+                width = NB // 2 if last else NB
+                for c in range(0, NB, width):
+                    c0 = NB * n + c
+                    acc = psum.tile([P, NB], F32, name="acc")
+                    for g in range(G):
+                        one_pass(acc[:, 0:width], x_op(g, t), w_op(g, c0, width), g)
+                    res = outs.tile([P, NB], F32, name="res")
+                    nc.vector.tensor_tensor(
+                        out=res[:, 0:width], in0=acc[:, 0:width], in1=update[n, t][:, c : c + width], op=ALU.subtract
+                    )
+                    nc.sync.dma_start(out=out[P * t : P * (t + 1), c0 : c0 + width], in_=res[:, 0:width])

@@ -18,7 +18,6 @@ G = IN // 512
 T = B // P
 NB = 512
 N_BLOCKS = OUT // NB
-WARM = 11
 
 
 def tile_optimizedlinear_kernel(
@@ -38,14 +37,16 @@ def tile_optimizedlinear_kernel(
             nc.sync.dma_start(out=dst.bitcast(I32), in_=src.bitcast(I32))
 
         def load_scales(plane, scales, g0, g1, c0, c1):
-            for q in range(4):
-                src = scales[g0:g1, 4 * q : 4 * q + 4, c0:c1].rearrange("g r n -> r g n")
-                nc.sync.dma_start(out=plane[32 * q : 32 * q + 4, :, :].bitcast(I32), in_=src.bitcast(I32))
+            for r in range(4):
+                src = scales[g0:g1, r : 16 : 4, c0:c1].rearrange("g q n -> q g n")
+                nc.sync.dma_start(out=plane[r : P : 32, :, :].bitcast(I32), in_=src.bitcast(I32))
 
         def zero(plane):
             nc.vector.memset(plane[:].rearrange("p g n -> p (g n)").bitcast(I32), 0)
 
         warm = keep_tile("warm", [P, NB], BF16)
+        rows = [keep_tile("prev_bias_rows", [P, NB], BF16), keep_tile("bias_rows", [P, NB], BF16)]
+        pick = keep_tile("pick", [P, N_BLOCKS, P], BF16)
         lr_bf = keep_tile("lr_bf", [P, T], BF16)
         lr_col = keep_tile("lr_col", [P, T], F32)
         spread = [keep_tile("prev_bias_b", [P, OUT], BF16), keep_tile("bias_b", [P, OUT], BF16)]
@@ -61,10 +62,16 @@ def tile_optimizedlinear_kernel(
         ysb = keep_tile("ysb", [P, G, NB], U8)
         ws = keep_tile("ws", [P, G, OUT], U8)
 
-        nc.gpsimd.memset(warm[:], 0.0)
+        nc.vector.memset(warm[:], 0.0)
+        for which, vec in enumerate((prev_bias, bias)):
+            nc.gpsimd.memset(rows[which][:], 0.0)
+            nc.scalar.dma_start(out=rows[which][0:96:32, :], in_=vec.rearrange("(n c) -> n c", c=NB))
+        nc.gpsimd.memset(pick[:], 0.0)
+        for n in range(N_BLOCKS):
+            nc.gpsimd.memset(pick[32 * n : 32 * n + 1, n, :], 1.0)
+        nc.gpsimd.dma_start(out=lr_bf[:], in_=lr.rearrange("(t p) -> p t", p=P))
         zero(ysa01)
         zero(xs)
-        nc.gpsimd.dma_start(out=lr_bf[:], in_=lr.rearrange("(t p) -> p t", p=P))
 
         load_codes(xc[0][:], x_words[0])
         load_codes(ya0[0][:], y_words[0][:, 0 : 2 * NB])
@@ -80,16 +87,6 @@ def tile_optimizedlinear_kernel(
         load_codes(xc35[:], x_words[3:6].rearrange("g p c -> p g c"))
         for g in (3, 4, 5):
             load_codes(ya[g][:], y_words[g][:, 0 : 4 * NB])
-        nc.sync.dma_start(out=spread[0][:], in_=prev_bias.partition_broadcast(P))
-        nc.sync.dma_start(out=spread[1][:], in_=bias.partition_broadcast(P))
-        zero(ysb)
-        load_scales(ysb, y_scales, 0, G, 2 * NB, 3 * NB)
-        load_codes(yb[:], y_words.rearrange("g p c -> p g c")[:, :, 4 * NB : 6 * NB])
-        zero(ws)
-        load_scales(ws, w_scales, 0, G, 0, OUT)
-        for g in range(G):
-            load_codes(wc[g][:], w_words[g])
-
         def x_op(g, t):
             codes = xc[g][:, 256 * t : 256 * (t + 1)] if g < 3 else xc35[:, g - 3, 256 * t : 256 * (t + 1)]
             return codes.bitcast(FP4X4), xs[:, g, P * t : P * (t + 1)]
@@ -115,11 +112,33 @@ def tile_optimizedlinear_kernel(
                 stop=(g == G - 1),
             )
 
-        nc.vector.tensor_copy(out=lr_col[:], in_=lr_bf[:])
-        acc = psum.tile([P, NB], F32, name="acc")
-        for i in range(WARM):
-            nc.tensor.matmul(out=acc[:], lhsT=warm[:, 0:P], rhs=warm[:], start=True, stop=True)
+        idle = psum.tile([P, NB], F32, name="acc")
 
+        def warm_up(count):
+            for i in range(count):
+                nc.tensor.matmul(out=idle[:], lhsT=warm[:, 0:P], rhs=warm[:], start=True, stop=True)
+
+        warm_up(4)
+        for which in range(2):
+            for n in range(N_BLOCKS):
+                acc = psum.tile([P, NB], F32, name="acc")
+                nc.tensor.matmul(out=acc[:], lhsT=pick[:, n, :], rhs=rows[which][:], start=True, stop=True)
+                dst = spread[which][:, NB * n : NB * (n + 1)]
+                if n % 2 == 0:
+                    nc.scalar.copy(out=dst, in_=acc[:])
+                else:
+                    nc.vector.tensor_copy(out=dst, in_=acc[:])
+        warm_up(2)
+
+        zero(ysb)
+        load_scales(ysb, y_scales, 0, G, 2 * NB, 3 * NB)
+        load_codes(yb[:], y_words.rearrange("g p c -> p g c")[:, :, 4 * NB : 6 * NB])
+        zero(ws)
+        load_scales(ws, w_scales, 0, G, 0, OUT)
+        for g in range(G):
+            load_codes(wc[g][:], w_words[g])
+
+        nc.vector.tensor_copy(out=lr_col[:], in_=lr_bf[:])
         shift = {}
         for n in range(N_BLOCKS):
             cols = slice(NB * n, NB * (n + 1))

@@ -18,6 +18,7 @@ G = IN // 512
 T = B // P
 NB = 512
 N_BLOCKS = OUT // NB
+ROW = OUT // 4
 
 
 def tile_optimizedlinear_kernel(
@@ -45,8 +46,8 @@ def tile_optimizedlinear_kernel(
             nc.vector.memset(plane[:].rearrange("p g n -> p (g n)").bitcast(I32), 0)
 
         warm = keep_tile("warm", [P, NB], BF16)
-        rows = [keep_tile("prev_bias_rows", [P, NB], BF16), keep_tile("bias_rows", [P, NB], BF16)]
-        pick = keep_tile("pick", [P, N_BLOCKS, P], BF16)
+        rows = [keep_tile("prev_bias_rows", [P, ROW], BF16), keep_tile("bias_rows", [P, ROW], BF16)]
+        pick = keep_tile("pick", [P, 4, P], BF16)
         lr_bf = keep_tile("lr_bf", [P, T], BF16)
         lr_col = keep_tile("lr_col", [P, T], F32)
         spread = [keep_tile("prev_bias_b", [P, OUT], BF16), keep_tile("bias_b", [P, OUT], BF16)]
@@ -62,12 +63,12 @@ def tile_optimizedlinear_kernel(
         ysb = keep_tile("ysb", [P, G, NB], U8)
         ws = keep_tile("ws", [P, G, OUT], U8)
 
-        nc.vector.memset(warm[:], 0.0)
+        nc.vector.memset(warm[:].bitcast(I32), 0)
         for which, vec in enumerate((prev_bias, bias)):
-            nc.gpsimd.memset(rows[which][:], 0.0)
-            nc.scalar.dma_start(out=rows[which][0:96:32, :], in_=vec.rearrange("(n c) -> n c", c=NB))
-        nc.gpsimd.memset(pick[:], 0.0)
-        for n in range(N_BLOCKS):
+            nc.gpsimd.memset(rows[which][:].bitcast(I32), 0)
+            nc.scalar.dma_start(out=rows[which][0:P:32, :], in_=vec.rearrange("(n c) -> n c", c=ROW))
+        nc.gpsimd.memset(pick[:].rearrange("p n c -> p (n c)").bitcast(I32), 0)
+        for n in range(4):
             nc.gpsimd.memset(pick[32 * n : 32 * n + 1, n, :], 1.0)
         nc.gpsimd.dma_start(out=lr_bf[:], in_=lr.rearrange("(t p) -> p t", p=P))
         zero(ysa01)
@@ -120,15 +121,14 @@ def tile_optimizedlinear_kernel(
 
         warm_up(4)
         for which in range(2):
-            for n in range(N_BLOCKS):
+            for n in range(4):
                 acc = psum.tile([P, NB], F32, name="acc")
-                nc.tensor.matmul(out=acc[:], lhsT=pick[:, n, :], rhs=rows[which][:], start=True, stop=True)
-                dst = spread[which][:, NB * n : NB * (n + 1)]
+                nc.tensor.matmul(out=acc[:, 0:ROW], lhsT=pick[:, n, :], rhs=rows[which][:], start=True, stop=True)
+                dst = spread[which][:, ROW * n : ROW * (n + 1)]
                 if n % 2 == 0:
-                    nc.scalar.copy(out=dst, in_=acc[:])
+                    nc.scalar.copy(out=dst, in_=acc[:, 0:ROW])
                 else:
-                    nc.vector.tensor_copy(out=dst, in_=acc[:])
-        warm_up(2)
+                    nc.vector.tensor_copy(out=dst, in_=acc[:, 0:ROW])
 
         zero(ysb)
         load_scales(ysb, y_scales, 0, G, 2 * NB, 3 * NB)

@@ -189,8 +189,8 @@ def tile_optimizedlinear_kernel(
         for n in range(N_BLOCKS):
             for t in range(T):
                 last = n == N_BLOCKS - 1 and t == T - 1
-                width = NB // 2 if last else NB
-                for c in range(0, NB, width):
+                c = 0
+                for width in (256, 128, 128) if last else (NB,):
                     c0 = NB * n + c
                     acc = psum.tile([P, NB], F32, name="acc")
                     for g in range(G):
@@ -200,3 +200,4 @@ def tile_optimizedlinear_kernel(
                         out=res[:, 0:width], in0=acc[:, 0:width], in1=update[n, t][:, c : c + width], op=ALU.subtract
                     )
                     nc.sync.dma_start(out=out[P * t : P * (t + 1), c0 : c0 + width], in_=res[:, 0:width])
+                    c += width

from contextlib import ExitStack

import concourse.mybir as mybir

F32 = mybir.dt.float32
BF16 = mybir.dt.bfloat16
U8 = mybir.dt.uint8
I32 = mybir.dt.int32
FP4X4 = mybir.dt.float4_e2m1fn_x4
ALU = mybir.AluOpType
ACT = mybir.ActivationFunctionType

B, IN, OUT = 512, 3072, 1536
FLOPS = 2 * 2 * B * IN * OUT

P = 128
G = IN // 512
T = B // P
NB = 512
N_BLOCKS = OUT // NB
ROW = OUT // 4


def tile_optimizedlinear_kernel(
    tc, x_words, x_scales, w_words, w_scales, bias, y_words, y_scales, prev_bias, lr, out
):
    nc = tc.nc
    with ExitStack() as ctx:
        keep = ctx.enter_context(tc.tile_pool(name="keep", bufs=1))
        outs = ctx.enter_context(tc.tile_pool(name="outs", bufs=6))
        psum = ctx.enter_context(tc.psum_pool(name="psum", bufs=8))
        ctx.enter_context(tc.manual_schedule())

        def keep_tile(name, shape, dtype):
            return keep.tile(shape, dtype, name=name, align_bytes=256)

        def load_codes(dst, src):
            nc.sync.dma_start(out=dst.bitcast(I32), in_=src.bitcast(I32))

        def load_scales(plane, scales, g0, g1, c0, c1):
            for r in range(4):
                src = scales[g0:g1, r : 16 : 4, c0:c1].rearrange("g q n -> q g n")
                nc.sync.dma_start(out=plane[r : P : 32, :, :].bitcast(I32), in_=src.bitcast(I32))

        def zero(plane):
            nc.vector.memset(plane[:].rearrange("p g n -> p (g n)").bitcast(I32), 0)

        warm = keep_tile("warm", [P, NB], BF16)
        rows = [keep_tile("prev_bias_rows", [P, ROW], BF16), keep_tile("bias_rows", [P, ROW], BF16)]
        pick = keep_tile("pick", [P, 4, P], BF16)
        lr_bf = keep_tile("lr_bf", [P, T], BF16)
        lr_col = keep_tile("lr_col", [P, T], F32)
        spread = [keep_tile("prev_bias_b", [P, OUT], BF16), keep_tile("bias_b", [P, OUT], BF16)]
        xc = [keep_tile("xc%d" % g, [P, 2 * B], U8) for g in range(3)]
        xc35 = keep_tile("xc35", [P, 3, 2 * B], U8)
        ya0 = [keep_tile("ya0_%d" % n, [P, 2 * NB], U8) for n in range(2)]
        ya = [None] + [keep_tile("ya%d" % g, [P, 4 * NB], U8) for g in range(1, G)]
        yb = keep_tile("yb", [P, G, 2 * NB], U8)
        wc = [keep_tile("wc%d" % g, [P, 2 * OUT], U8) for g in range(G)]
        xs = keep_tile("xs", [P, G, B], U8)
        ysa01 = keep_tile("ysa01", [P, 2, 2 * NB], U8)
        ysa25 = keep_tile("ysa25", [P, 4, 2 * NB], U8)
        ysb = keep_tile("ysb", [P, G, NB], U8)
        ws = keep_tile("ws", [P, G, OUT], U8)

        nc.vector.memset(warm[:].bitcast(I32), 0)
        for which, vec in enumerate((prev_bias, bias)):
            nc.gpsimd.memset(rows[which][:].bitcast(I32), 0)
            nc.scalar.dma_start(out=rows[which][0:P:32, :], in_=vec.rearrange("(n c) -> n c", c=ROW))
        nc.gpsimd.memset(pick[:].rearrange("p n c -> p (n c)").bitcast(I32), 0)
        for n in range(4):
            nc.gpsimd.memset(pick[32 * n : 32 * n + 1, n, :], 1.0)
        nc.gpsimd.dma_start(out=lr_bf[:], in_=lr.rearrange("(t p) -> p t", p=P))
        zero(ysa01)
        zero(xs)

        load_codes(xc[0][:], x_words[0])
        load_codes(ya0[0][:], y_words[0][:, 0 : 2 * NB])
        load_scales(ysa01, y_scales, 0, 2, 0, 2 * NB)
        load_scales(xs, x_scales, 0, G, 0, B)
        load_codes(ya0[1][:], y_words[0][:, 2 * NB : 4 * NB])
        load_codes(xc[1][:], x_words[1])
        load_codes(ya[1][:], y_words[1][:, 0 : 4 * NB])
        zero(ysa25)
        load_scales(ysa25, y_scales, 2, G, 0, 2 * NB)
        load_codes(xc[2][:], x_words[2])
        load_codes(ya[2][:], y_words[2][:, 0 : 4 * NB])
        load_codes(xc35[:], x_words[3:6].rearrange("g p c -> p g c"))
        for g in (3, 4, 5):
            load_codes(ya[g][:], y_words[g][:, 0 : 4 * NB])
        def x_op(g, t):
            codes = xc[g][:, 256 * t : 256 * (t + 1)] if g < 3 else xc35[:, g - 3, 256 * t : 256 * (t + 1)]
            return codes.bitcast(FP4X4), xs[:, g, P * t : P * (t + 1)]

        def y_op(g, n):
            if n == 2:
                return yb[:, g, :].bitcast(FP4X4), ysb[:, g, :]
            codes = ya0[n][:] if g == 0 else ya[g][:, 2 * NB * n : 2 * NB * (n + 1)]
            plane = ysa01[:, g, NB * n : NB * (n + 1)] if g < 2 else ysa25[:, g - 2, NB * n : NB * (n + 1)]
            return codes.bitcast(FP4X4), plane

        def w_op(g, c0, width):
            return wc[g][:, 2 * c0 : 2 * (c0 + width)].bitcast(FP4X4), ws[:, g, c0 : c0 + width]

        def one_pass(acc, stationary, moving, g):
            nc.tensor.matmul_mx(
                out=acc,
                lhsT=stationary[0],
                lhsT_scale=stationary[1],
                rhs=moving[0],
                rhs_scale=moving[1],
                start=(g == 0),
                stop=(g == G - 1),
            )

        idle = psum.tile([P, NB], F32, name="acc")

        def warm_up(count):
            for i in range(count):
                nc.tensor.matmul(out=idle[:], lhsT=warm[:, 0:P], rhs=warm[:], start=True, stop=True)

        warm_up(4)
        for which in range(2):
            for n in range(4):
                acc = psum.tile([P, NB], F32, name="acc")
                nc.tensor.matmul(out=acc[:, 0:ROW], lhsT=pick[:, n, :], rhs=rows[which][:], start=True, stop=True)
                dst = spread[which][:, ROW * n : ROW * (n + 1)]
                if n % 2 == 0:
                    nc.scalar.copy(out=dst, in_=acc[:, 0:ROW])
                else:
                    nc.vector.tensor_copy(out=dst, in_=acc[:, 0:ROW])

        zero(ysb)
        load_scales(ysb, y_scales, 0, G, 2 * NB, 3 * NB)
        load_codes(yb[:], y_words.rearrange("g p c -> p g c")[:, :, 4 * NB : 6 * NB])
        zero(ws)
        load_scales(ws, w_scales, 0, G, 0, OUT)
        for g in range(G):
            load_codes(wc[g][:], w_words[g])

        nc.vector.tensor_copy(out=lr_col[:], in_=lr_bf[:])
        shift = {}
        for n in range(N_BLOCKS):
            cols = slice(NB * n, NB * (n + 1))
            for t in range(T):
                s = keep_tile("shift%d_%d" % (n, t), [P, NB], F32)
                nc.vector.scalar_tensor_tensor(
                    out=s[:],
                    in0=spread[0][:, cols],
                    scalar=lr_col[:, t : t + 1],
                    in1=spread[1][:, cols],
                    op0=ALU.mult,
                    op1=ALU.subtract,
                )
                shift[n, t] = s

        update = {}

        def finish_pert(acc, n, t):
            u = keep_tile("update%d_%d" % (n, t), [P, NB], F32)
            nc.vector.scalar_tensor_tensor(
                out=u[:],
                in0=acc[:],
                scalar=lr_col[:, t : t + 1],
                in1=shift[n, t][:],
                op0=ALU.mult,
                op1=ALU.add,
            )
            update[n, t] = u

        first = [(n, t) for n in range(2) for t in range(T)]
        accs = {}
        for g in range(4):
            for n, t in first:
                if g == 0:
                    acc = psum.tile([P, NB], F32, name="acc")
                    accs[n, t] = acc
                one_pass(accs[n, t][:], x_op(g, t), y_op(g, n), g)
        for n, t in first:
            for g in range(4, G):
                one_pass(accs[n, t][:], x_op(g, t), y_op(g, n), g)
            finish_pert(accs[n, t], n, t)
        for t in range(T):
            acc = psum.tile([P, NB], F32, name="acc")
            for g in range(G):
                one_pass(acc[:], x_op(g, t), y_op(g, 2), g)
            finish_pert(acc, 2, t)

        for n in range(N_BLOCKS):
            for t in range(T):
                last = n == N_BLOCKS - 1 and t == T - 1
                c = 0
                for width in (256, 128, 128) if last else (NB,):
                    c0 = NB * n + c
                    acc = psum.tile([P, NB], F32, name="acc")
                    for g in range(G):
                        one_pass(acc[:, 0:width], x_op(g, t), w_op(g, c0, width), g)
                    res = outs.tile([P, NB], F32, name="res")
                    nc.vector.tensor_tensor(
                        out=res[:, 0:width], in0=acc[:, 0:width], in1=update[n, t][:, c : c + width], op=ALU.subtract
                    )
                    nc.sync.dma_start(out=out[P * t : P * (t + 1), c0 : c0 + width], in_=res[:, 0:width])
                    c += width
